import numpy as np
import ml_dtypes


def mxq(x, axis, fmt="e4m3"):
    dtype, down = {"e4m3": (ml_dtypes.float8_e4m3fn, 7), "e5m2": (ml_dtypes.float8_e5m2, 14)}[fmt]
    v = np.moveaxis(np.asarray(x, np.float32).astype(ml_dtypes.bfloat16).astype(np.float64), axis, -1)
    blocks = v.reshape(v.shape[:-1] + (-1, 32))
    amax = np.abs(blocks).max(-1, keepdims=True)
    byte = np.maximum(np.where(amax > 0, np.frexp(amax)[1] - 1 + 127, 0) - down, 1)
    scale = np.exp2(byte - 127.0)
    codes = (blocks / scale).astype(np.float32).astype(dtype).astype(np.float64)
    return np.moveaxis((codes * scale).reshape(v.shape), -1, axis)


WIDE = False


def mx_kscale(k):
    if not WIDE:
        return np.ones(k)
    levels = np.array([10, -10, 5, -5, 0])
    if k % 512:
        return np.exp2(np.random.permutation(np.resize(levels, k // 32))).repeat(32)
    a = np.empty((k // 512, 16))
    for p in range(k // 512):
        a[p, :8] = np.random.permutation(np.resize(levels, 8))
        for g in range(8):
            far = levels[np.abs(levels - a[p, g]) >= 10]
            a[p, g + 8] = far[np.random.randint(len(far))]
    return np.exp2(a.ravel()).repeat(32)


BF16 = ml_dtypes.bfloat16


def bf(x):
    return np.asarray(x, np.float32).astype(BF16)


def f64(x):
    return np.asarray(x).astype(np.float64)


B, L, M, E, H, D, FW = 1, 512, 512, 512, 8, 512, 4
EPS = 1e-5


def layer_norm(x, g, b):
    m = x.mean(-1, keepdims=True)
    v = ((x - m) ** 2).mean(-1, keepdims=True)
    return (x - m) / np.sqrt(v + EPS) * g + b


def setup_inputs():
    s, t = mx_kscale(E), mx_kscale(D)
    return {"q": bf(np.random.standard_normal((B, L, E)) * 0.5 + 0.25),
            "g1": bf((1.0 + 0.1 * np.random.standard_normal(E)) * s),
            "be1": bf(0.1 * np.random.standard_normal(E) * s),
            "Wq_s": bf(np.random.standard_normal((H, E, D)) * 1.4 / np.sqrt(E) / s[:, None] * t),
            "Wk_s": bf(np.random.standard_normal((H, E, D)) * 1.4 / np.sqrt(E) / s[:, None] / t)}


def reference(q, g1, be1, Wq_s, Wk_s):
    xq = mxq(layer_norm(f64(q), f64(g1), f64(be1)), 2, "e4m3")
    wq = mxq(f64(Wq_s).transpose(1, 0, 2).reshape(E, H * D), 0, "e4m3")
    wk = mxq(f64(Wk_s).transpose(1, 0, 2).reshape(E, H * D), 0, "e4m3")
    Q = (xq @ wq).reshape(B, L, H, D).transpose(0, 2, 1, 3)
    K = (xq @ wk).reshape(B, L, H, D).transpose(0, 2, 1, 3)
    return (mxq(Q, 3, "e4m3") @ mxq(K, 3, "e4m3").transpose(0, 1, 3, 2)) * D ** -0.5

from contextlib import ExitStack

import concourse.mybir as mybir
from concourse.masks import make_identity

F32 = mybir.dt.float32
BF16 = mybir.dt.bfloat16
U32 = mybir.dt.uint32
U8 = mybir.dt.uint8
FP8X4 = mybir.dt.float8_e4m3fn_x4
ACT = mybir.ActivationFunctionType
ALU = mybir.AluOpType

P = 128
PACK = 4
HEADS = 8
L = 512
E = 512
D = 512
LT = L // P
UNITS = 2 * HEADS
EPS = 1e-5
OUT_SCALE = D ** -0.5
FLOPS = 2 * L * E * 2 * HEADS * D + 2 * HEADS * L * L * D

V_R1 = lambda i: (3,) if i < 4 else (1, 3)
V_RT = lambda i: ()
V_R2 = lambda h: {6: (0, 1), 7: (1, 3)}.get(h, ())
S_WINT = (2,)
WPREP = lambda i: [i + 3] if i + 3 <= UNITS else []
S2_AT = lambda i: [((i - 3 - k) // 2, 2 * k + j) for k in (0, 1) for j in (0, 1) if (i - 3 - k) % 2 == 0 and 0 <= (i - 3 - k) // 2 < HEADS]


def tile_decoderlayer_pb_kernel(tc, q, g1, be1, Wq_s, Wk_s, out):
    nc = tc.nc
    with ExitStack() as ctx:
        const = ctx.enter_context(tc.tile_pool(name="const", bufs=1))
        wraw = ctx.enter_context(tc.tile_pool(name="wraw", bufs=UNITS))
        wgrp = ctx.enter_context(tc.tile_pool(name="wgrp", bufs=4))
        wcod = ctx.enter_context(tc.tile_pool(name="wcod", bufs=16))
        natp = ctx.enter_context(tc.tile_pool(name="natp", bufs=3))
        grpp = ctx.enter_context(tc.tile_pool(name="grpp", bufs=3))
        zcod = ctx.enter_context(tc.tile_pool(name="zcod", bufs=6))
        ostp = ctx.enter_context(tc.tile_pool(name="ostp", bufs=10))
        psum = ctx.enter_context(tc.psum_pool(name="psum", bufs=8))
        ctx.enter_context(tc.manual_schedule())

        raw, wg, wc, ws, nat, grp, zc, zs = {}, {}, {}, {}, {}, {}, {}, {}

        def copy_on(vector):
            return nc.vector.tensor_copy if vector else nc.scalar.copy

        qs = const.tile([P, LT, E], BF16, name="qs")
        for a in range(LT):
            nc.sync.dma_start(out=qs[:, a, :], in_=q[0, a * P:(a + 1) * P, :])
        g_bf = const.tile([P, PACK], BF16, name="g_bf")
        b_bf = const.tile([P, PACK], BF16, name="b_bf")
        nc.scalar.dma_start(out=g_bf[:], in_=g1.rearrange("(p t) -> p t", t=PACK))
        nc.scalar.dma_start(out=b_bf[:], in_=be1.rearrange("(p t) -> p t", t=PACK))
        for i in range(UNITS):
            w = (Wk_s, Wq_s)[i % 2]
            raw[i] = wraw.tile([P, PACK, D], BF16, name="raw", tag="raw")
            nc.sync.dma_start(out=raw[i][:], in_=w[i // 2].rearrange("(p j) d -> p j d", j=PACK))

        def interleave(vector, dst, src):
            copy_on(vector)(out=dst.rearrange("p (c i j) -> p c j i", i=4, j=PACK),
                            in_=src.rearrange("p j (c i) -> p c j i", i=4))

        def w_interleave(i):
            wg[i] = wgrp.tile([P, PACK * D], BF16, name="wg", tag="wg", align_bytes=64)
            interleave(i not in S_WINT, wg[i][:], raw[i][:])

        def w_quant(i):
            wc[i] = wcod.tile([P, D], U32, name="wc", tag="wc", align_bytes=64)
            ws[i] = wcod.tile([P, D], U8, name="ws", tag="ws", align_bytes=64)
            nc.vector.quantize_mx(out=wc[i][:].bitcast(FP8X4), scales=ws[i][:], in_=wg[i][:])

        def stage1(i):
            nat[i] = natp.tile([P, LT, D], BF16, name="nat", tag="nat")
            for a in range(LT):
                bank = psum.tile([P, D], F32, tag="bank")
                cols = slice(a * P, (a + 1) * P)
                nc.tensor.matmul_mx(out=bank[:], lhsT=xc[:, cols].bitcast(FP8X4), lhsT_scale=xsc[:, cols],
                                    rhs=wc[i][:].bitcast(FP8X4), rhs_scale=ws[i][:], start=True, stop=True)
                copy_on(a in V_R1(i))(out=nat[i][:, a, :].rearrange("p (u m e) -> p u m e", u=2, e=2),
                                      in_=bank[:].rearrange("p (m u e) -> p u m e", u=2, e=2))

        def turn(i):
            grp[i] = grpp.tile([P, PACK * L], BF16, name="grp", tag="grp", align_bytes=64)
            words = grp[i][:].bitcast(F32)
            for b in range(2):
                xt = psum.tile([P, 512], F32, tag="bank")
                for a2 in range(2):
                    nw = nat[i][:, 2 * b + a2, :].bitcast(F32)
                    for u in range(2):
                        nc.tensor.transpose(xt[:, u * 256 + a2 * P: u * 256 + (a2 + 1) * P], nw[:, u * P:(u + 1) * P], ident[:])
                copy_on(b in V_RT(i))(out=words[:, b * 512:(b + 1) * 512].rearrange("p (r u) -> p r u", u=2),
                                      in_=xt[:].rearrange("p (u r) -> p r u", u=2))

        def z_quant(i):
            zc[i] = zcod.tile([P, L], U32, name="zc", tag="zc", align_bytes=64)
            zs[i] = zcod.tile([P, L], U8, name="zs", tag="zs", align_bytes=64)
            for c0, c1 in (((0, L),), ((0, L // 2), (L // 2, L)))[i % 2]:
                nc.vector.quantize_mx(out=zc[i][:, c0:c1].bitcast(FP8X4), scales=zs[i][:, c0:c1], in_=grp[i][:, PACK * c0:PACK * c1])

        def stage2(h, a):
            bank = psum.tile([P, L], F32, tag="bank")
            cols = slice(a * P, (a + 1) * P)
            nc.tensor.matmul_mx(out=bank[:], lhsT=zc[2 * h + 1][:, cols].bitcast(FP8X4), lhsT_scale=zs[2 * h + 1][:, cols],
                                rhs=zc[2 * h][:].bitcast(FP8X4), rhs_scale=zs[2 * h][:], start=True, stop=True)
            ost = ostp.tile([P, L], F32, tag="ost")
            if a in V_R2(h):
                nc.vector.tensor_scalar_mul(out=ost[:], in0=bank[:], scalar1=OUT_SCALE)
            else:
                nc.scalar.activation(out=ost[:], in_=bank[:], func=ACT.Copy, scale=OUT_SCALE)
            nc.sync.dma_start(out=out[0, h, cols, :], in_=ost[:])

        eps = const.tile([P, 1], F32, name="eps")
        nc.vector.memset(eps[:], EPS)
        warm = const.tile([P, 1], F32, name="warm")
        nc.scalar.activation(out=warm[:], in_=eps[:], func=ACT.Sqrt)
        ident = const.tile([P, P], F32, name="ident")
        make_identity(nc, ident[:])

        st = const.tile([P, LT, 6], F32, name="st")
        mv = const.tile([P, LT, 2], F32, name="mv")
        for a in range(LT):
            nc.vector.bn_stats(out=st[:, a, :], in_=qs[:, a, :])
            nc.vector.bn_aggr(out=mv[:, a, :], in_=st[:, a, :])
        sd = const.tile([P, LT], F32, name="sd")
        nc.scalar.activation(out=sd[:], in_=mv[:, :, 1], func=ACT.Sqrt, bias=eps[:])
        rstd = const.tile([P, LT], F32, name="rstd")
        nc.vector.reciprocal(out=rstd[:], in_=sd[:])
        nmr = const.tile([P, LT], F32, name="nmr")
        nc.vector.scalar_tensor_tensor(out=nmr[:], in0=mv[:, :, 0], scalar=-1.0, in1=rstd[:], op0=ALU.mult, op1=ALU.mult)

        xn = const.tile([P, LT, E], F32, name="xn")
        for a in (0, 2, 1, 3):
            dst = xn[:, a, :].rearrange("l (t p) -> l t p", t=PACK)
            src = qs[:, a, :].rearrange("l (p t) -> l t p", t=PACK)
            if a < 2:
                nc.vector.tensor_scalar(out=dst, in0=src, scalar1=mv[:, a, 0:1], scalar2=rstd[:, a:a + 1], op0=ALU.subtract, op1=ALU.mult)
            else:
                nc.scalar.activation(out=dst, in_=src, func=ACT.Identity, bias=nmr[:, a:a + 1], scale=rstd[:, a:a + 1])
        gb = const.tile([P, 2 * PACK], F32, name="gb")
        nc.vector.tensor_copy(out=gb[:, 0:PACK], in_=g_bf[:])
        nc.vector.tensor_copy(out=gb[:, PACK:2 * PACK], in_=b_bf[:])
        w_interleave(0)
        xT = []
        for t in range(PACK):
            xT_t = psum.tile([P, L], F32, tag="bank")
            xT.append(xT_t)
        for a in (0, 2, 1, 3):
            for t in range(PACK):
                nc.tensor.transpose(xT[t][:, a * P:(a + 1) * P], xn[:, a, t * P:(t + 1) * P], ident[:])
        xs = const.tile([P, PACK, L], BF16, name="xs")
        for t in (0, 2, 1, 3):
            if t < 2:
                nc.scalar.activation(out=xs[:, t, :], in_=xT[t][:], func=ACT.Identity, bias=gb[:, PACK + t:PACK + t + 1], scale=gb[:, t:t + 1])
            else:
                nc.vector.tensor_scalar(out=xs[:, t, :], in0=xT[t][:], scalar1=gb[:, t:t + 1], scalar2=gb[:, PACK + t:PACK + t + 1], op0=ALU.mult, op1=ALU.add)
        xg = const.tile([P, PACK * L], BF16, name="xg", align_bytes=64)
        xc = const.tile([P, L], U32, name="xc", align_bytes=64)
        xsc = const.tile([P, L], U8, name="xsc", align_bytes=64)
        for half in range(2):
            interleave(half == 0, xg[:, half * 2 * L:(half + 1) * 2 * L], xs[:, :, half * L // 2:(half + 1) * L // 2])
        w_quant(0)
        for half in range(2):
            cols = slice(half * L // 2, (half + 1) * L // 2)
            nc.vector.quantize_mx(out=xc[:, cols].bitcast(FP8X4), scales=xsc[:, cols], in_=xg[:, half * 2 * L:(half + 1) * 2 * L])
        w_interleave(1)
        w_quant(1)
        w_interleave(2)

        for i in range(UNITS + 3):
            if i < UNITS:
                stage1(i)
            for h, a in S2_AT(i):
                stage2(h, a)
            if i < UNITS:
                turn(i)
            if 1 <= i <= UNITS:
                z_quant(i - 1)
            for n in WPREP(i):
                if n < UNITS:
                    w_interleave(n)
                w_quant(n - 1)
